import numpy as np
import ml_dtypes


def mxq(x, axis, fmt="e4m3"):
    dtype, down = {"e4m3": (ml_dtypes.float8_e4m3fn, 7), "e5m2": (ml_dtypes.float8_e5m2, 14)}[fmt]
    v = np.moveaxis(np.asarray(x, np.float32).astype(ml_dtypes.bfloat16).astype(np.float64), axis, -1)
    blocks = v.reshape(v.shape[:-1] + (-1, 32))
    amax = np.abs(blocks).max(-1, keepdims=True)
    byte = np.maximum(np.where(amax > 0, np.frexp(amax)[1] - 1 + 127, 0) - down, 1)
    scale = np.exp2(byte - 127.0)
    codes = (blocks / scale).astype(np.float32).astype(dtype).astype(np.float64)
    return np.moveaxis((codes * scale).reshape(v.shape), -1, axis)


WIDE = False


def mx_kscale(k):
    if not WIDE:
        return np.ones(k)
    levels = np.array([10, -10, 5, -5, 0])
    a = np.random.permutation(np.resize(levels, k // 512 * 4)).reshape(k // 512, 4)
    idx = np.arange(k)
    return np.exp2(a[idx // 512, idx % 128 // 32])


BF16 = ml_dtypes.bfloat16


def bf(x):
    return np.asarray(x, np.float32).astype(BF16)


def f64(x):
    return np.asarray(x).astype(np.float64)


B, DIN, H1, H2, N, I, K, O = 256, 2048, 16384, 512, 32, 16, 256, 16
NI = N * I
LN_EPS = 1e-5


def setup_inputs():
    s, t = mx_kscale(H1), mx_kscale(H2)
    return {"h1": bf(np.maximum(np.random.standard_normal((B, H1)), 0.0) * s),
            "W2": bf(np.random.standard_normal((H1, H2)) * 1.4 / np.sqrt(H1) / s[:, None] * t),
            "b2": bf(np.random.standard_normal(H2) * 0.2 * t),
            "Wp": bf(np.random.standard_normal((N, H2, I)) * 1.4 / np.sqrt(H2) / t[None, :, None]),
            "bp": bf(np.random.standard_normal((N, I)) * 0.2),
            "ln_g": bf(1.0 + 0.1 * np.random.standard_normal((N, I))),
            "ln_b": bf(0.1 * np.random.standard_normal((N, I)))}


def reference(h1, W2, b2, Wp, bp, ln_g, ln_b):
    x = np.maximum((mxq(f64(h1), 1, "e4m3") @ mxq(f64(W2), 0, "e4m3")) + f64(b2), 0.0)
    wpf = f64(Wp).transpose(1, 0, 2).reshape(H2, NI)
    p = (mxq(x, 1, "e4m3") @ mxq(wpf, 0, "e4m3")).reshape(B, N, I) + f64(bp)
    mu = p.mean(-1, keepdims=True)
    var = ((p - mu) ** 2).mean(-1, keepdims=True)
    return (p - mu) / np.sqrt(var + LN_EPS) * f64(ln_g) + f64(ln_b)

@@ -1,0 +1,343 @@
+from contextlib import ExitStack
+
+import concourse.mybir as mybir
+from concourse.masks import make_identity
+
+F32 = mybir.dt.float32
+BF16 = mybir.dt.bfloat16
+U32 = mybir.dt.uint32
+U8 = mybir.dt.uint8
+FP8X4 = mybir.dt.float8_e4m3fn_x4
+ACT = mybir.ActivationFunctionType
+ALU = mybir.AluOpType
+AXIS = mybir.AxisListType
+
+BATCH, H1, H2, CAPS, CAP_DIM = 256, 16384, 512, 32, 16
+NI = CAPS * CAP_DIM
+LN_EPS = 1e-5
+FLOPS = 2 * BATCH * H1 * H2 + 2 * BATCH * H2 * NI
+
+P = 128
+PACK = 4
+K_PASS = P * PACK
+PASSES = H1 // K_PASS
+ROW_BLOCKS = BATCH // P
+WORD_HALVES = 2
+WORDS = K_PASS // WORD_HALVES
+I_PER_BANK = 8
+
+W2_LOAD_PASSES = 2
+H1_LOAD_PASSES = 4
+W2_LOADS = PASSES // W2_LOAD_PASSES
+H1_LOADS = PASSES // H1_LOAD_PASSES
+W2_BUFS = 8
+H1_BUFS = W2_BUFS * W2_LOAD_PASSES // H1_LOAD_PASSES
+VECTOR_COLS = 288
+
+
+def tile_capsulenetwork_pa_k_kernel(tc, h1, W2, b2, Wp, bp, ln_g, ln_b, out):
+    nc = tc.nc
+    with ExitStack() as ctx:
+        const = ctx.enter_context(tc.tile_pool(name="const", bufs=1))
+        w2_in = ctx.enter_context(tc.tile_pool(name="w2_in", bufs=W2_BUFS))
+        h1_in = ctx.enter_context(tc.tile_pool(name="h1_in", bufs=H1_BUFS))
+        grouped_pool = ctx.enter_context(tc.tile_pool(name="grouped", bufs=3))
+        codes_pool = ctx.enter_context(tc.tile_pool(name="codes", bufs=4))
+        norm_pool = ctx.enter_context(tc.tile_pool(name="norm", bufs=ROW_BLOCKS))
+        acc_pool = ctx.enter_context(tc.psum_pool(name="acc", bufs=1))
+        bank_pool = ctx.enter_context(tc.psum_pool(name="bank", bufs=4))
+        ctx.enter_context(tc.manual_schedule())
+
+        w2_raw = {}
+        h1_raw = {}
+        h1_banks = {}
+        w2_grouped, h1_grouped = {}, {}
+        w2_codes, w2_scales, h1_codes, h1_scales = {}, {}, {}, {}
+
+        def load_w2(n):
+            if n >= W2_LOADS:
+                return
+            rows = W2[n * W2_LOAD_PASSES * K_PASS : (n + 1) * W2_LOAD_PASSES * K_PASS, :]
+            w2_raw[n] = w2_in.tile([P, W2_LOAD_PASSES * PACK * H2], BF16, name="w2_raw")
+            nc.sync.dma_start(
+                out=w2_raw[n][:].rearrange("p (g r) -> p g r", g=W2_LOAD_PASSES),
+                in_=rows.rearrange("(g p j) n -> p g (j n)", g=W2_LOAD_PASSES, j=PACK),
+            )
+
+        def load_h1(n):
+            if n >= H1_LOADS:
+                return
+            cols = h1[:, n * H1_LOAD_PASSES * K_PASS : (n + 1) * H1_LOAD_PASSES * K_PASS]
+            h1_raw[n] = h1_in.tile([P, ROW_BLOCKS * H1_LOAD_PASSES * K_PASS], BF16, name="h1_raw")
+            nc.sync.dma_start(
+                out=h1_raw[n][:].rearrange("p (blk k) -> p blk k", blk=ROW_BLOCKS),
+                in_=cols.rearrange("(blk p) k -> p blk k", p=P),
+            )
+
+        ident_f32 = const.tile([P, P], F32)
+        make_identity(nc, ident_f32[:])
+        ident_bf16 = const.tile([P, P], BF16)
+        make_identity(nc, ident_bf16[:])
+        ones = const.tile([P, P], BF16)
+        nc.vector.memset(ones[:], 1.0)
+        eps = const.tile([P, 1], F32)
+        nc.vector.memset(eps[:], LN_EPS)
+
+        vector_rows = const.tile([P, 3 * NI], BF16)
+        nc.vector.memset(vector_rows[:], 0.0)
+        for i, vec in enumerate((bp, ln_g, ln_b)):
+            nc.scalar.dma_start(
+                out=vector_rows[0:1, i * NI : (i + 1) * NI], in_=vec.rearrange("(o n) i -> o (n i)", o=1)
+            )
+        b2_rows = const.tile([P, P], BF16)
+        nc.vector.memset(b2_rows[:], 0.0)
+        nc.scalar.dma_start(out=b2_rows[0:PACK, :], in_=b2.rearrange("(t p) -> t p", p=P))
+
+        sqrt_first = const.tile([P, 1], F32)
+        nc.scalar.activation(out=sqrt_first[:], in_=eps[:], func=ACT.Sqrt)
+
+        spread_banks = []
+        spread = const.tile([P, 3 * NI], BF16)
+        bp_all, g_all, b_all = [spread[:, i * NI : (i + 1) * NI] for i in range(3)]
+        b2_col = const.tile([P, PACK], F32)
+
+        def spread_vectors():
+            for bank in range(2):
+                spread_banks.append(bank_pool.tile([P, 2 * NI], BF16, name="spread_bank", tag="bank"))
+            for i in range(3):
+                nc.tensor.matmul(
+                    out=spread_banks[i // 2][:, (i % 2) * NI : (i % 2 + 1) * NI],
+                    lhsT=ones[:],
+                    rhs=vector_rows[:, i * NI : (i + 1) * NI],
+                    start=True,
+                    stop=True,
+                )
+            nc.tensor.transpose(spread_banks[1][:, NI : NI + P], b2_rows[:], ident_bf16[:])
+
+        def keep_vectors():
+            nc.scalar.copy(out=spread[:, : 2 * NI], in_=spread_banks[0][:])
+            nc.scalar.copy(out=spread[:, 2 * NI :], in_=spread_banks[1][:, :NI])
+            nc.scalar.copy(out=b2_col[:], in_=spread_banks[1][:, NI : NI + PACK])
+
+        wp_raw = const.tile([P, P * CAP_DIM], BF16)
+        for n in range(W2_BUFS):
+            load_w2(n)
+            if n * W2_LOAD_PASSES % H1_LOAD_PASSES == 0:
+                load_h1(n * W2_LOAD_PASSES // H1_LOAD_PASSES)
+            if n == 0:
+                nc.sync.dma_start(
+                    out=wp_raw[:], in_=Wp.rearrange("n (t p) i -> (n t) (p i)", t=PACK, p=P)
+                )
+
+        wp_banks = []
+        wp_grouped = const.tile([P, NI * PACK], BF16, align_bytes=64)
+        wp_codes = const.tile([P, NI], U32, align_bytes=64)
+        wp_scales = const.tile([P, NI], U8, align_bytes=64)
+
+        def transpose_wp():
+            wp_by_i = wp_raw[:].rearrange("c (p i) -> c i p", i=CAP_DIM)
+            for first_i in range(0, CAP_DIM, I_PER_BANK):
+                wp_bank = bank_pool.tile([P, I_PER_BANK * P], BF16, tag="bank")
+                for i in range(I_PER_BANK):
+                    nc.tensor.transpose(
+                        wp_bank[:, i * P : (i + 1) * P], wp_by_i[:, first_i + i, :], ident_bf16[:]
+                    )
+                wp_banks.append(wp_bank)
+
+        def regroup_wp():
+            by_cap = wp_grouped[:].rearrange("p (n i t) -> p n i t", i=CAP_DIM, t=PACK)
+            for half, wp_bank in enumerate(wp_banks):
+                nc.scalar.copy(
+                    out=by_cap[:, :, half * I_PER_BANK : (half + 1) * I_PER_BANK, :],
+                    in_=wp_bank[:].rearrange("p (i n t) -> p n i t", i=I_PER_BANK, t=PACK),
+                )
+
+        def quantise_wp():
+            nc.vector.quantize_mx(
+                out=wp_codes[:].bitcast(FP8X4), scales=wp_scales[:], in_=wp_grouped[:]
+            )
+
+        def transpose_h1(g):
+            words = h1_raw[g // H1_LOAD_PASSES][:].bitcast(F32)
+            h1_banks[g] = bank_pool.tile([P, ROW_BLOCKS * WORD_HALVES * P], F32, name="h1_bank", tag="bank")
+            for blk in range(ROW_BLOCKS):
+                first = (blk * H1_LOAD_PASSES + g % H1_LOAD_PASSES) * WORDS
+                for u in range(WORD_HALVES):
+                    plane = (blk * WORD_HALVES + u) * P
+                    nc.tensor.transpose(
+                        h1_banks[g][:, plane : plane + P],
+                        words[:, first + u : first + WORDS : WORD_HALVES],
+                        ident_f32[:],
+                    )
+
+        def regroup_h1(g):
+            h1_grouped[g] = grouped_pool.tile([P, BATCH * PACK], BF16, name="h1_grouped", align_bytes=64)
+            nc.scalar.copy(
+                out=h1_grouped[g][:].bitcast(F32).rearrange(
+                    "p (blk r u) -> p blk r u", blk=ROW_BLOCKS, u=WORD_HALVES
+                ),
+                in_=h1_banks[g][:].rearrange("p (blk u r) -> p blk r u", blk=ROW_BLOCKS, u=WORD_HALVES),
+            )
+
+        def regroup_w2(g):
+            first = (g % W2_LOAD_PASSES) * PACK * H2
+            raw = w2_raw[g // W2_LOAD_PASSES][:, first : first + PACK * H2].rearrange("p (j n) -> p j n", j=PACK)
+            w2_grouped[g] = grouped_pool.tile([P, H2 * PACK], BF16, name="w2_grouped", align_bytes=64)
+            nc.vector.tensor_copy(
+                out=w2_grouped[g][:, : VECTOR_COLS * PACK].rearrange("p (c i j) -> p c j i", i=4, j=PACK),
+                in_=raw[:, :, :VECTOR_COLS].rearrange("p j (c i) -> p c j i", i=4),
+            )
+            nc.scalar.copy(
+                out=w2_grouped[g][:, VECTOR_COLS * PACK :].rearrange("p (c i j) -> p c j i", i=4, j=PACK),
+                in_=raw[:, :, VECTOR_COLS:].rearrange("p j (c i) -> p c j i", i=4),
+            )
+
+        def quantise(g):
+            w2_codes[g] = codes_pool.tile([P, H2], U32, name="w2_codes", align_bytes=64)
+            w2_scales[g] = codes_pool.tile([P, H2], U8, name="w2_scales", align_bytes=64)
+            nc.vector.quantize_mx(
+                out=w2_codes[g][:].bitcast(FP8X4), scales=w2_scales[g][:], in_=w2_grouped[g][:]
+            )
+            h1_codes[g] = codes_pool.tile([P, BATCH], U32, name="h1_codes", align_bytes=64)
+            h1_scales[g] = codes_pool.tile([P, BATCH], U8, name="h1_scales", align_bytes=64)
+            nc.vector.quantize_mx(
+                out=h1_codes[g][:].bitcast(FP8X4), scales=h1_scales[g][:], in_=h1_grouped[g][:]
+            )
+
+        sums = [acc_pool.tile([P, BATCH], F32, name="sums%d" % t) for t in range(PACK)]
+
+        def multiply(g):
+            for t in range(PACK):
+                cols = slice(t * P, (t + 1) * P)
+                nc.tensor.matmul_mx(
+                    out=sums[t][:],
+                    lhsT=w2_codes[g][:, cols].bitcast(FP8X4),
+                    lhsT_scale=w2_scales[g][:, cols],
+                    rhs=h1_codes[g][:].bitcast(FP8X4),
+                    rhs_scale=h1_scales[g][:],
+                    start=(g == 0),
+                    stop=(g == PASSES - 1),
+                )
+
+        def stream_step(s):
+            if s % 2 == 0 and s < PASSES:
+                transpose_h1(s)
+                transpose_h1(s + 1)
+                if (s + 2) % H1_LOAD_PASSES == 0:
+                    load_h1(s // H1_LOAD_PASSES + H1_BUFS)
+            if s < PASSES:
+                regroup_w2(s)
+                regroup_h1(s)
+                if (s + 1) % W2_LOAD_PASSES == 0:
+                    load_w2(s // W2_LOAD_PASSES + W2_BUFS)
+            if 1 <= s <= PASSES:
+                quantise(s - 1)
+            if s % 2 == 1 and s >= 3:
+                multiply(s - 3)
+                multiply(s - 2)
+
+        def stream_steps(first, end):
+            for s in range(first, end):
+                stream_step(s)
+
+        stream_steps(0, 2)
+        spread_vectors()
+        stream_steps(2, 4)
+        keep_vectors()
+        transpose_wp()
+        stream_steps(4, 5)
+        regroup_wp()
+        stream_steps(5, 6)
+        quantise_wp()
+        stream_steps(6, PASSES + 2)
+
+        x_planes = const.tile([P, PACK * BATCH], BF16)
+        for t in range(PACK):
+            plane = x_planes[:, t * BATCH : (t + 1) * BATCH]
+            if t % 2 == 0:
+                nc.scalar.activation(out=plane, in_=sums[t][:], func=ACT.Relu, bias=b2_col[:, t : t + 1])
+            else:
+                nc.vector.tensor_scalar(
+                    out=plane, in0=sums[t][:], scalar1=b2_col[:, t : t + 1], scalar2=0.0,
+                    op0=ALU.add, op1=ALU.max,
+                )
+        x_grouped = const.tile([P, BATCH * PACK], BF16, align_bytes=64)
+        nc.vector.tensor_copy(
+            out=x_grouped[:].rearrange("p (b t) -> p b t", t=PACK),
+            in_=x_planes[:].rearrange("p (t b) -> p b t", t=PACK),
+        )
+        x_codes = const.tile([P, BATCH], U32, align_bytes=64)
+        x_scales = const.tile([P, BATCH], U8, align_bytes=64)
+        nc.vector.quantize_mx(out=x_codes[:].bitcast(FP8X4), scales=x_scales[:], in_=x_grouped[:])
+
+        def by_cap(ap):
+            return ap.rearrange("p (n i) -> p n i", i=CAP_DIM)
+
+        def over_cap(ap):
+            return ap.unsqueeze(2).to_broadcast([P, CAPS, CAP_DIM])
+
+        norm = {}
+
+        def norm_tile(name, m, cols):
+            norm[name, m] = norm_pool.tile([P, cols], F32, name=name)
+            return norm[name, m][:]
+
+        blocks = range(ROW_BLOCKS)
+        product = {}
+        for m in blocks:
+            product[m] = bank_pool.tile([P, NI], F32, name="product", tag="bank")
+            rows = slice(m * P, (m + 1) * P)
+            nc.tensor.matmul_mx(
+                out=product[m][:],
+                lhsT=x_codes[:, rows].bitcast(FP8X4),
+                lhsT_scale=x_scales[:, rows],
+                rhs=wp_codes[:].bitcast(FP8X4),
+                rhs_scale=wp_scales[:],
+                start=True,
+                stop=True,
+            )
+        for m in blocks:
+            nc.vector.tensor_tensor(out=norm_tile("u", m, NI), in0=product[m][:], in1=bp_all, op=ALU.add)
+        for m in blocks:
+            nc.vector.tensor_reduce(
+                out=norm_tile("total", m, CAPS), in_=by_cap(norm["u", m][:]), axis=AXIS.X, op=ALU.add
+            )
+        for m in blocks:
+            nc.vector.scalar_tensor_tensor(
+                out=by_cap(norm_tile("dev", m, NI)),
+                in0=over_cap(norm["total", m][:]),
+                scalar=-1.0 / CAP_DIM,
+                in1=by_cap(norm["u", m][:]),
+                op0=ALU.mult,
+                op1=ALU.add,
+            )
+        for m in blocks:
+            nc.scalar.activation(out=norm_tile("dev_sq", m, NI), in_=norm["dev", m][:], func=ACT.Square)
+        for m in blocks:
+            nc.vector.tensor_tensor(
+                out=norm_tile("dev_g", m, NI), in0=norm["dev", m][:], in1=g_all, op=ALU.mult
+            )
+        for m in blocks:
+            nc.vector.tensor_reduce(
+                out=norm_tile("sq_total", m, CAPS), in_=by_cap(norm["dev_sq", m][:]), axis=AXIS.X, op=ALU.add
+            )
+        for m in blocks:
+            nc.scalar.activation(
+                out=norm_tile("std", m, CAPS), in_=norm["sq_total", m][:], func=ACT.Sqrt,
+                scale=1.0 / CAP_DIM, bias=eps[:],
+            )
+        for m in blocks:
+            nc.vector.reciprocal(out=norm_tile("inv_std", m, CAPS), in_=norm["std", m][:])
+        for m in blocks:
+            nc.vector.tensor_tensor(
+                out=by_cap(norm_tile("scaled", m, NI)),
+                in0=by_cap(norm["dev_g", m][:]),
+                in1=over_cap(norm["inv_std", m][:]),
+                op=ALU.mult,
+            )
+        out_rows = out.rearrange("b n i -> b (n i)")
+        for m in blocks:
+            nc.vector.tensor_tensor(
+                out=norm_tile("result", m, NI), in0=norm["scaled", m][:], in1=b_all, op=ALU.add
+            )
+            nc.sync.dma_start(out=out_rows[m * P : (m + 1) * P, :], in_=norm["result", m][:])

@@ -26,12 +26,10 @@ WORD_HALVES = 2
 WORDS = K_PASS // WORD_HALVES
 I_PER_BANK = 8
 
-W2_LOAD_PASSES = 2
 H1_LOAD_PASSES = 4
-W2_LOADS = PASSES // W2_LOAD_PASSES
 H1_LOADS = PASSES // H1_LOAD_PASSES
-W2_BUFS = 8
-H1_BUFS = W2_BUFS * W2_LOAD_PASSES // H1_LOAD_PASSES
+W2_BUFS = 16
+H1_BUFS = W2_BUFS // H1_LOAD_PASSES
 VECTOR_COLS = 288
 
 
@@ -43,6 +41,7 @@ def tile_capsulenetwork_pa_k_kernel(tc, h1, W2, b2, Wp, bp, ln_g, ln_b, out):
         h1_in = ctx.enter_context(tc.tile_pool(name="h1_in", bufs=H1_BUFS))
         grouped_pool = ctx.enter_context(tc.tile_pool(name="grouped", bufs=3))
         codes_pool = ctx.enter_context(tc.tile_pool(name="codes", bufs=4))
+        h1_codes_pool = ctx.enter_context(tc.tile_pool(name="h1_codes", bufs=6))
         norm_pool = ctx.enter_context(tc.tile_pool(name="norm", bufs=ROW_BLOCKS))
         acc_pool = ctx.enter_context(tc.psum_pool(name="acc", bufs=1))
         bank_pool = ctx.enter_context(tc.psum_pool(name="bank", bufs=4))
@@ -54,14 +53,13 @@ def tile_capsulenetwork_pa_k_kernel(tc, h1, W2, b2, Wp, bp, ln_g, ln_b, out):
         w2_grouped, h1_grouped = {}, {}
         w2_codes, w2_scales, h1_codes, h1_scales = {}, {}, {}, {}
 
-        def load_w2(n):
-            if n >= W2_LOADS:
+        def load_w2(g):
+            if g >= PASSES:
                 return
-            rows = W2[n * W2_LOAD_PASSES * K_PASS : (n + 1) * W2_LOAD_PASSES * K_PASS, :]
-            w2_raw[n] = w2_in.tile([P, W2_LOAD_PASSES * PACK * H2], BF16, name="w2_raw")
+            w2_raw[g] = w2_in.tile([P, PACK * H2], BF16, name="w2_raw")
             nc.sync.dma_start(
-                out=w2_raw[n][:].rearrange("p (g r) -> p g r", g=W2_LOAD_PASSES),
-                in_=rows.rearrange("(g p j) n -> p g (j n)", g=W2_LOAD_PASSES, j=PACK),
+                out=w2_raw[g][:],
+                in_=W2[g * K_PASS : (g + 1) * K_PASS, :].rearrange("(p j) n -> p (j n)", j=PACK),
             )
 
         def load_h1(n):
@@ -120,11 +118,11 @@ def tile_capsulenetwork_pa_k_kernel(tc, h1, W2, b2, Wp, bp, ln_g, ln_b, out):
             nc.scalar.copy(out=b2_col[:], in_=spread_banks[1][:, NI : NI + PACK])
 
         wp_raw = const.tile([P, P * CAP_DIM], BF16)
-        for n in range(W2_BUFS):
-            load_w2(n)
-            if n * W2_LOAD_PASSES % H1_LOAD_PASSES == 0:
-                load_h1(n * W2_LOAD_PASSES // H1_LOAD_PASSES)
-            if n == 0:
+        for g in range(W2_BUFS):
+            load_w2(g)
+            if g % H1_LOAD_PASSES == 0:
+                load_h1(g // H1_LOAD_PASSES)
+            if g == H1_LOAD_PASSES - 1:
                 nc.sync.dma_start(
                     out=wp_raw[:], in_=Wp.rearrange("n (t p) i -> (n t) (p i)", t=PACK, p=P)
                 )
@@ -180,8 +178,7 @@ def tile_capsulenetwork_pa_k_kernel(tc, h1, W2, b2, Wp, bp, ln_g, ln_b, out):
             )
 
         def regroup_w2(g):
-            first = (g % W2_LOAD_PASSES) * PACK * H2
-            raw = w2_raw[g // W2_LOAD_PASSES][:, first : first + PACK * H2].rearrange("p (j n) -> p j n", j=PACK)
+            raw = w2_raw[g][:].rearrange("p (j n) -> p j n", j=PACK)
             w2_grouped[g] = grouped_pool.tile([P, H2 * PACK], BF16, name="w2_grouped", align_bytes=64)
             nc.vector.tensor_copy(
                 out=w2_grouped[g][:, : VECTOR_COLS * PACK].rearrange("p (c i j) -> p c j i", i=4, j=PACK),
@@ -192,14 +189,16 @@ def tile_capsulenetwork_pa_k_kernel(tc, h1, W2, b2, Wp, bp, ln_g, ln_b, out):
                 in_=raw[:, :, VECTOR_COLS:].rearrange("p j (c i) -> p c j i", i=4),
             )
 
-        def quantise(g):
+        def quantise_w2(g):
             w2_codes[g] = codes_pool.tile([P, H2], U32, name="w2_codes", align_bytes=64)
             w2_scales[g] = codes_pool.tile([P, H2], U8, name="w2_scales", align_bytes=64)
             nc.vector.quantize_mx(
                 out=w2_codes[g][:].bitcast(FP8X4), scales=w2_scales[g][:], in_=w2_grouped[g][:]
             )
-            h1_codes[g] = codes_pool.tile([P, BATCH], U32, name="h1_codes", align_bytes=64)
-            h1_scales[g] = codes_pool.tile([P, BATCH], U8, name="h1_scales", align_bytes=64)
+
+        def quantise_h1(g):
+            h1_codes[g] = h1_codes_pool.tile([P, BATCH], U32, name="h1_codes", align_bytes=64)
+            h1_scales[g] = h1_codes_pool.tile([P, BATCH], U8, name="h1_scales", align_bytes=64)
             nc.vector.quantize_mx(
                 out=h1_codes[g][:].bitcast(FP8X4), scales=h1_scales[g][:], in_=h1_grouped[g][:]
             )
@@ -219,19 +218,26 @@ def tile_capsulenetwork_pa_k_kernel(tc, h1, W2, b2, Wp, bp, ln_g, ln_b, out):
                     stop=(g == PASSES - 1),
                 )
 
+        def transpose_pair(g):
+            if g >= PASSES:
+                return
+            transpose_h1(g)
+            transpose_h1(g + 1)
+            if (g + 2) % H1_LOAD_PASSES == 0:
+                load_h1(g // H1_LOAD_PASSES + H1_BUFS)
+
         def stream_step(s):
-            if s % 2 == 0 and s < PASSES:
-                transpose_h1(s)
-                transpose_h1(s + 1)
-                if (s + 2) % H1_LOAD_PASSES == 0:
-                    load_h1(s // H1_LOAD_PASSES + H1_BUFS)
+            if s % 2 == 0:
+                transpose_pair(s + 2)
             if s < PASSES:
                 regroup_w2(s)
-                regroup_h1(s)
-                if (s + 1) % W2_LOAD_PASSES == 0:
-                    load_w2(s // W2_LOAD_PASSES + W2_BUFS)
+                load_w2(s + W2_BUFS)
+            if s + 1 < PASSES:
+                regroup_h1(s + 1)
             if 1 <= s <= PASSES:
-                quantise(s - 1)
+                quantise_w2(s - 1)
+            if s < PASSES:
+                quantise_h1(s)
             if s % 2 == 1 and s >= 3:
                 multiply(s - 3)
                 multiply(s - 2)
@@ -240,6 +246,8 @@ def tile_capsulenetwork_pa_k_kernel(tc, h1, W2, b2, Wp, bp, ln_g, ln_b, out):
             for s in range(first, end):
                 stream_step(s)
 
+        transpose_pair(0)
+        regroup_h1(0)
         stream_steps(0, 2)
         spread_vectors()
         stream_steps(2, 4)
@@ -314,7 +322,7 @@ def tile_capsulenetwork_pa_k_kernel(tc, h1, W2, b2, Wp, bp, ln_g, ln_b, out):
         for m in blocks:
             nc.scalar.activation(out=norm_tile("dev_sq", m, NI), in_=norm["dev", m][:], func=ACT.Square)
         for m in blocks:
-            nc.vector.tensor_tensor(
+            nc.gpsimd.tensor_tensor(
                 out=norm_tile("dev_g", m, NI), in0=norm["dev", m][:], in1=g_all, op=ALU.mult
             )
         for m in blocks:

@@ -218,35 +218,29 @@ def tile_capsulenetwork_pa_k_kernel(tc, h1, W2, b2, Wp, bp, ln_g, ln_b, out):
                     stop=(g == PASSES - 1),
                 )
 
-        def transpose_pair(g):
-            if g >= PASSES:
-                return
-            transpose_h1(g)
-            transpose_h1(g + 1)
-            if (g + 2) % H1_LOAD_PASSES == 0:
-                load_h1(g // H1_LOAD_PASSES + H1_BUFS)
-
         def stream_step(s):
-            if s % 2 == 0:
-                transpose_pair(s + 2)
+            if s + 2 < PASSES:
+                transpose_h1(s + 2)
+                if (s + 3) % H1_LOAD_PASSES == 0:
+                    load_h1((s + 2) // H1_LOAD_PASSES + H1_BUFS)
             if s < PASSES:
                 regroup_w2(s)
                 load_w2(s + W2_BUFS)
             if s + 1 < PASSES:
                 regroup_h1(s + 1)
-            if 1 <= s <= PASSES:
+            if s >= 1:
                 quantise_w2(s - 1)
             if s < PASSES:
                 quantise_h1(s)
-            if s % 2 == 1 and s >= 3:
-                multiply(s - 3)
-                multiply(s - 2)
+            if s >= 1:
+                multiply(s - 1)
 
         def stream_steps(first, end):
             for s in range(first, end):
                 stream_step(s)
 
-        transpose_pair(0)
+        transpose_h1(0)
+        transpose_h1(1)
         regroup_h1(0)
         stream_steps(0, 2)
         spread_vectors()
@@ -257,7 +251,7 @@ def tile_capsulenetwork_pa_k_kernel(tc, h1, W2, b2, Wp, bp, ln_g, ln_b, out):
         regroup_wp()
         stream_steps(5, 6)
         quantise_wp()
-        stream_steps(6, PASSES + 2)
+        stream_steps(6, PASSES + 1)
 
         x_planes = const.tile([P, PACK * BATCH], BF16)
         for t in range(PACK):

from contextlib import ExitStack

import concourse.mybir as mybir
from concourse.masks import make_identity

F32 = mybir.dt.float32
BF16 = mybir.dt.bfloat16
U32 = mybir.dt.uint32
U8 = mybir.dt.uint8
FP8X4 = mybir.dt.float8_e4m3fn_x4
ACT = mybir.ActivationFunctionType
ALU = mybir.AluOpType
AXIS = mybir.AxisListType

BATCH, H1, H2, CAPS, CAP_DIM = 256, 16384, 512, 32, 16
NI = CAPS * CAP_DIM
LN_EPS = 1e-5
FLOPS = 2 * BATCH * H1 * H2 + 2 * BATCH * H2 * NI

P = 128
PACK = 4
K_PASS = P * PACK
PASSES = H1 // K_PASS
ROW_BLOCKS = BATCH // P
WORD_HALVES = 2
WORDS = K_PASS // WORD_HALVES
I_PER_BANK = 8

H1_LOAD_PASSES = 4
H1_LOADS = PASSES // H1_LOAD_PASSES
W2_BUFS = 16
H1_BUFS = W2_BUFS // H1_LOAD_PASSES
VECTOR_COLS = 288


def tile_capsulenetwork_pa_k_kernel(tc, h1, W2, b2, Wp, bp, ln_g, ln_b, out):
    nc = tc.nc
    with ExitStack() as ctx:
        const = ctx.enter_context(tc.tile_pool(name="const", bufs=1))
        w2_in = ctx.enter_context(tc.tile_pool(name="w2_in", bufs=W2_BUFS))
        h1_in = ctx.enter_context(tc.tile_pool(name="h1_in", bufs=H1_BUFS))
        grouped_pool = ctx.enter_context(tc.tile_pool(name="grouped", bufs=3))
        codes_pool = ctx.enter_context(tc.tile_pool(name="codes", bufs=4))
        h1_codes_pool = ctx.enter_context(tc.tile_pool(name="h1_codes", bufs=6))
        norm_pool = ctx.enter_context(tc.tile_pool(name="norm", bufs=ROW_BLOCKS))
        acc_pool = ctx.enter_context(tc.psum_pool(name="acc", bufs=1))
        bank_pool = ctx.enter_context(tc.psum_pool(name="bank", bufs=4))
        ctx.enter_context(tc.manual_schedule())

        w2_raw = {}
        h1_raw = {}
        h1_banks = {}
        w2_grouped, h1_grouped = {}, {}
        w2_codes, w2_scales, h1_codes, h1_scales = {}, {}, {}, {}

        def load_w2(g):
            if g >= PASSES:
                return
            w2_raw[g] = w2_in.tile([P, PACK * H2], BF16, name="w2_raw")
            nc.sync.dma_start(
                out=w2_raw[g][:],
                in_=W2[g * K_PASS : (g + 1) * K_PASS, :].rearrange("(p j) n -> p (j n)", j=PACK),
            )

        def load_h1(n):
            if n >= H1_LOADS:
                return
            cols = h1[:, n * H1_LOAD_PASSES * K_PASS : (n + 1) * H1_LOAD_PASSES * K_PASS]
            h1_raw[n] = h1_in.tile([P, ROW_BLOCKS * H1_LOAD_PASSES * K_PASS], BF16, name="h1_raw")
            nc.sync.dma_start(
                out=h1_raw[n][:].rearrange("p (blk k) -> p blk k", blk=ROW_BLOCKS),
                in_=cols.rearrange("(blk p) k -> p blk k", p=P),
            )

        ident_f32 = const.tile([P, P], F32)
        make_identity(nc, ident_f32[:])
        ident_bf16 = const.tile([P, P], BF16)
        make_identity(nc, ident_bf16[:])
        ones = const.tile([P, P], BF16)
        nc.vector.memset(ones[:], 1.0)
        eps = const.tile([P, 1], F32)
        nc.vector.memset(eps[:], LN_EPS)

        vector_rows = const.tile([P, 3 * NI], BF16)
        nc.vector.memset(vector_rows[:], 0.0)
        for i, vec in enumerate((bp, ln_g, ln_b)):
            nc.scalar.dma_start(
                out=vector_rows[0:1, i * NI : (i + 1) * NI], in_=vec.rearrange("(o n) i -> o (n i)", o=1)
            )
        b2_rows = const.tile([P, P], BF16)
        nc.vector.memset(b2_rows[:], 0.0)
        nc.scalar.dma_start(out=b2_rows[0:PACK, :], in_=b2.rearrange("(t p) -> t p", p=P))

        sqrt_first = const.tile([P, 1], F32)
        nc.scalar.activation(out=sqrt_first[:], in_=eps[:], func=ACT.Sqrt)

        spread_banks = []
        spread = const.tile([P, 3 * NI], BF16)
        bp_all, g_all, b_all = [spread[:, i * NI : (i + 1) * NI] for i in range(3)]
        b2_col = const.tile([P, PACK], F32)

        def spread_vectors():
            for bank in range(2):
                spread_banks.append(bank_pool.tile([P, 2 * NI], BF16, name="spread_bank", tag="bank"))
            for i in range(3):
                nc.tensor.matmul(
                    out=spread_banks[i // 2][:, (i % 2) * NI : (i % 2 + 1) * NI],
                    lhsT=ones[:],
                    rhs=vector_rows[:, i * NI : (i + 1) * NI],
                    start=True,
                    stop=True,
                )
            nc.tensor.transpose(spread_banks[1][:, NI : NI + P], b2_rows[:], ident_bf16[:])

        def keep_vectors():
            nc.scalar.copy(out=spread[:, : 2 * NI], in_=spread_banks[0][:])
            nc.scalar.copy(out=spread[:, 2 * NI :], in_=spread_banks[1][:, :NI])
            nc.scalar.copy(out=b2_col[:], in_=spread_banks[1][:, NI : NI + PACK])

        wp_raw = const.tile([P, P * CAP_DIM], BF16)
        for g in range(W2_BUFS):
            load_w2(g)
            if g % H1_LOAD_PASSES == 0:
                load_h1(g // H1_LOAD_PASSES)
            if g == H1_LOAD_PASSES - 1:
                nc.sync.dma_start(
                    out=wp_raw[:], in_=Wp.rearrange("n (t p) i -> (n t) (p i)", t=PACK, p=P)
                )

        wp_banks = []
        wp_grouped = const.tile([P, NI * PACK], BF16, align_bytes=64)
        wp_codes = const.tile([P, NI], U32, align_bytes=64)
        wp_scales = const.tile([P, NI], U8, align_bytes=64)

        def transpose_wp():
            wp_by_i = wp_raw[:].rearrange("c (p i) -> c i p", i=CAP_DIM)
            for first_i in range(0, CAP_DIM, I_PER_BANK):
                wp_bank = bank_pool.tile([P, I_PER_BANK * P], BF16, tag="bank")
                for i in range(I_PER_BANK):
                    nc.tensor.transpose(
                        wp_bank[:, i * P : (i + 1) * P], wp_by_i[:, first_i + i, :], ident_bf16[:]
                    )
                wp_banks.append(wp_bank)

        def regroup_wp():
            by_cap = wp_grouped[:].rearrange("p (n i t) -> p n i t", i=CAP_DIM, t=PACK)
            for half, wp_bank in enumerate(wp_banks):
                nc.scalar.copy(
                    out=by_cap[:, :, half * I_PER_BANK : (half + 1) * I_PER_BANK, :],
                    in_=wp_bank[:].rearrange("p (i n t) -> p n i t", i=I_PER_BANK, t=PACK),
                )

        def quantise_wp():
            nc.vector.quantize_mx(
                out=wp_codes[:].bitcast(FP8X4), scales=wp_scales[:], in_=wp_grouped[:]
            )

        def transpose_h1(g):
            words = h1_raw[g // H1_LOAD_PASSES][:].bitcast(F32)
            h1_banks[g] = bank_pool.tile([P, ROW_BLOCKS * WORD_HALVES * P], F32, name="h1_bank", tag="bank")
            for blk in range(ROW_BLOCKS):
                first = (blk * H1_LOAD_PASSES + g % H1_LOAD_PASSES) * WORDS
                for u in range(WORD_HALVES):
                    plane = (blk * WORD_HALVES + u) * P
                    nc.tensor.transpose(
                        h1_banks[g][:, plane : plane + P],
                        words[:, first + u : first + WORDS : WORD_HALVES],
                        ident_f32[:],
                    )

        def regroup_h1(g):
            h1_grouped[g] = grouped_pool.tile([P, BATCH * PACK], BF16, name="h1_grouped", align_bytes=64)
            nc.scalar.copy(
                out=h1_grouped[g][:].bitcast(F32).rearrange(
                    "p (blk r u) -> p blk r u", blk=ROW_BLOCKS, u=WORD_HALVES
                ),
                in_=h1_banks[g][:].rearrange("p (blk u r) -> p blk r u", blk=ROW_BLOCKS, u=WORD_HALVES),
            )

        def regroup_w2(g):
            raw = w2_raw[g][:].rearrange("p (j n) -> p j n", j=PACK)
            w2_grouped[g] = grouped_pool.tile([P, H2 * PACK], BF16, name="w2_grouped", align_bytes=64)
            nc.vector.tensor_copy(
                out=w2_grouped[g][:, : VECTOR_COLS * PACK].rearrange("p (c i j) -> p c j i", i=4, j=PACK),
                in_=raw[:, :, :VECTOR_COLS].rearrange("p j (c i) -> p c j i", i=4),
            )
            nc.scalar.copy(
                out=w2_grouped[g][:, VECTOR_COLS * PACK :].rearrange("p (c i j) -> p c j i", i=4, j=PACK),
                in_=raw[:, :, VECTOR_COLS:].rearrange("p j (c i) -> p c j i", i=4),
            )

        def quantise_w2(g):
            w2_codes[g] = codes_pool.tile([P, H2], U32, name="w2_codes", align_bytes=64)
            w2_scales[g] = codes_pool.tile([P, H2], U8, name="w2_scales", align_bytes=64)
            nc.vector.quantize_mx(
                out=w2_codes[g][:].bitcast(FP8X4), scales=w2_scales[g][:], in_=w2_grouped[g][:]
            )

        def quantise_h1(g):
            h1_codes[g] = h1_codes_pool.tile([P, BATCH], U32, name="h1_codes", align_bytes=64)
            h1_scales[g] = h1_codes_pool.tile([P, BATCH], U8, name="h1_scales", align_bytes=64)
            nc.vector.quantize_mx(
                out=h1_codes[g][:].bitcast(FP8X4), scales=h1_scales[g][:], in_=h1_grouped[g][:]
            )

        sums = [acc_pool.tile([P, BATCH], F32, name="sums%d" % t) for t in range(PACK)]

        def multiply(g):
            for t in range(PACK):
                cols = slice(t * P, (t + 1) * P)
                nc.tensor.matmul_mx(
                    out=sums[t][:],
                    lhsT=w2_codes[g][:, cols].bitcast(FP8X4),
                    lhsT_scale=w2_scales[g][:, cols],
                    rhs=h1_codes[g][:].bitcast(FP8X4),
                    rhs_scale=h1_scales[g][:],
                    start=(g == 0),
                    stop=(g == PASSES - 1),
                )

        def stream_step(s):
            if s + 2 < PASSES:
                transpose_h1(s + 2)
                if (s + 3) % H1_LOAD_PASSES == 0:
                    load_h1((s + 2) // H1_LOAD_PASSES + H1_BUFS)
            if s < PASSES:
                regroup_w2(s)
                load_w2(s + W2_BUFS)
            if s + 1 < PASSES:
                regroup_h1(s + 1)
            if s >= 1:
                quantise_w2(s - 1)
            if s < PASSES:
                quantise_h1(s)
            if s >= 1:
                multiply(s - 1)

        def stream_steps(first, end):
            for s in range(first, end):
                stream_step(s)

        transpose_h1(0)
        transpose_h1(1)
        regroup_h1(0)
        stream_steps(0, 2)
        spread_vectors()
        stream_steps(2, 4)
        keep_vectors()
        transpose_wp()
        stream_steps(4, 5)
        regroup_wp()
        stream_steps(5, 6)
        quantise_wp()
        stream_steps(6, PASSES + 1)

        x_planes = const.tile([P, PACK * BATCH], BF16)
        for t in range(PACK):
            plane = x_planes[:, t * BATCH : (t + 1) * BATCH]
            if t % 2 == 0:
                nc.scalar.activation(out=plane, in_=sums[t][:], func=ACT.Relu, bias=b2_col[:, t : t + 1])
            else:
                nc.vector.tensor_scalar(
                    out=plane, in0=sums[t][:], scalar1=b2_col[:, t : t + 1], scalar2=0.0,
                    op0=ALU.add, op1=ALU.max,
                )
        x_grouped = const.tile([P, BATCH * PACK], BF16, align_bytes=64)
        nc.vector.tensor_copy(
            out=x_grouped[:].rearrange("p (b t) -> p b t", t=PACK),
            in_=x_planes[:].rearrange("p (t b) -> p b t", t=PACK),
        )
        x_codes = const.tile([P, BATCH], U32, align_bytes=64)
        x_scales = const.tile([P, BATCH], U8, align_bytes=64)
        nc.vector.quantize_mx(out=x_codes[:].bitcast(FP8X4), scales=x_scales[:], in_=x_grouped[:])

        def by_cap(ap):
            return ap.rearrange("p (n i) -> p n i", i=CAP_DIM)

        def over_cap(ap):
            return ap.unsqueeze(2).to_broadcast([P, CAPS, CAP_DIM])

        norm = {}

        def norm_tile(name, m, cols):
            norm[name, m] = norm_pool.tile([P, cols], F32, name=name)
            return norm[name, m][:]

        blocks = range(ROW_BLOCKS)
        product = {}
        for m in blocks:
            product[m] = bank_pool.tile([P, NI], F32, name="product", tag="bank")
            rows = slice(m * P, (m + 1) * P)
            nc.tensor.matmul_mx(
                out=product[m][:],
                lhsT=x_codes[:, rows].bitcast(FP8X4),
                lhsT_scale=x_scales[:, rows],
                rhs=wp_codes[:].bitcast(FP8X4),
                rhs_scale=wp_scales[:],
                start=True,
                stop=True,
            )
        for m in blocks:
            nc.vector.tensor_tensor(out=norm_tile("u", m, NI), in0=product[m][:], in1=bp_all, op=ALU.add)
        for m in blocks:
            nc.vector.tensor_reduce(
                out=norm_tile("total", m, CAPS), in_=by_cap(norm["u", m][:]), axis=AXIS.X, op=ALU.add
            )
        for m in blocks:
            nc.vector.scalar_tensor_tensor(
                out=by_cap(norm_tile("dev", m, NI)),
                in0=over_cap(norm["total", m][:]),
                scalar=-1.0 / CAP_DIM,
                in1=by_cap(norm["u", m][:]),
                op0=ALU.mult,
                op1=ALU.add,
            )
        for m in blocks:
            nc.scalar.activation(out=norm_tile("dev_sq", m, NI), in_=norm["dev", m][:], func=ACT.Square)
        for m in blocks:
            nc.gpsimd.tensor_tensor(
                out=norm_tile("dev_g", m, NI), in0=norm["dev", m][:], in1=g_all, op=ALU.mult
            )
        for m in blocks:
            nc.vector.tensor_reduce(
                out=norm_tile("sq_total", m, CAPS), in_=by_cap(norm["dev_sq", m][:]), axis=AXIS.X, op=ALU.add
            )
        for m in blocks:
            nc.scalar.activation(
                out=norm_tile("std", m, CAPS), in_=norm["sq_total", m][:], func=ACT.Sqrt,
                scale=1.0 / CAP_DIM, bias=eps[:],
            )
        for m in blocks:
            nc.vector.reciprocal(out=norm_tile("inv_std", m, CAPS), in_=norm["std", m][:])
        for m in blocks:
            nc.vector.tensor_tensor(
                out=by_cap(norm_tile("scaled", m, NI)),
                in0=by_cap(norm["dev_g", m][:]),
                in1=over_cap(norm["inv_std", m][:]),
                op=ALU.mult,
            )
        out_rows = out.rearrange("b n i -> b (n i)")
        for m in blocks:
            nc.vector.tensor_tensor(
                out=norm_tile("result", m, NI), in0=norm["scaled", m][:], in1=b_all, op=ALU.add
            )
            nc.sync.dma_start(out=out_rows[m * P : (m + 1) * P, :], in_=norm["result", m][:])
